import numpy as np
import ml_dtypes


def mxq(x, axis, fmt="e4m3"):
    dtype, down = {"e4m3": (ml_dtypes.float8_e4m3fn, 7), "e5m2": (ml_dtypes.float8_e5m2, 14)}[fmt]
    v = np.moveaxis(np.asarray(x, np.float32).astype(ml_dtypes.bfloat16).astype(np.float64), axis, -1)
    blocks = v.reshape(v.shape[:-1] + (-1, 32))
    amax = np.abs(blocks).max(-1, keepdims=True)
    byte = np.maximum(np.where(amax > 0, np.frexp(amax)[1] - 1 + 127, 0) - down, 1)
    scale = np.exp2(byte - 127.0)
    codes = (blocks / scale).astype(np.float32).astype(dtype).astype(np.float64)
    return np.moveaxis((codes * scale).reshape(v.shape), -1, axis)


WIDE = False


def mx_kscale(k):
    if not WIDE:
        return np.ones(k)
    levels = np.array([10, -10, 5, -5, 0])
    a = np.random.permutation(np.resize(levels, k // 512 * 4)).reshape(k // 512, 4)
    idx = np.arange(k)
    return np.exp2(a[idx // 512, idx % 128 // 32])


BF16 = ml_dtypes.bfloat16


def bf(x):
    return np.asarray(x, np.float32).astype(BF16)


def f64(x):
    return np.asarray(x).astype(np.float64)


B, F0, FK, S1, S2, D = 8, 8, 128, 128, 1024, 16
M1 = F0 * FK
M2 = F0 * S1


def setup_inputs():
    u = mx_kscale(M2).reshape(F0, S1)[:, 0]
    t = mx_kscale(M1).reshape(F0, FK)[0]
    w1 = np.random.standard_normal((F0, FK, S1)) / np.sqrt(M1) / u[:, None, None] / t[None, :, None]
    w2 = np.random.standard_normal((F0, S1, S2)) / np.sqrt(M2) / u[:, None, None]
    return {"x": bf(np.random.standard_normal((B, F0, D)) * u[None, :, None]),
            "x1": bf(np.random.standard_normal((B, FK, D)) * t[None, :, None]),
            "w1": bf(w1.reshape(M1, S1)), "b1": bf(np.random.standard_normal(S1) * 0.2),
            "w2": bf(w2.reshape(M2, S2)), "b2": bf(np.random.standard_normal(S2) * 0.2)}


def reference(x, x1, w1, b1, w2, b2):
    x0 = f64(x).transpose(0, 2, 1)
    xk = f64(x1).transpose(0, 2, 1)
    z1 = (x0[:, :, :, None] * xk[:, :, None, :]).reshape(B, D, M1)
    o1 = (mxq(z1, 2, "e4m3") @ mxq(f64(w1), 0, "e4m3")) + f64(b1)
    z2 = (x0[:, :, :, None] * o1[:, :, None, :]).reshape(B, D, M2)
    o2 = (mxq(z2, 2, "e4m3") @ mxq(f64(w2), 0, "e4m3")) + f64(b2)
    return np.concatenate([o1.sum(axis=1), o2.sum(axis=1)], axis=1)

@@ -1,0 +1,208 @@
+from contextlib import ExitStack
+
+import concourse.mybir as mybir
+from concourse.masks import make_identity
+
+BF16 = mybir.dt.bfloat16
+F32 = mybir.dt.float32
+U32 = mybir.dt.uint32
+U8 = mybir.dt.uint8
+FP8X4 = mybir.dt.float8_e4m3fn_x4
+ADD = mybir.AluOpType.add
+MULT = mybir.AluOpType.mult
+
+P = 128
+PACK = 4
+B, F0, FK, S1, S2, D = 8, 8, 128, 128, 1024, 16
+TOK = B * D
+PASSES = F0 // PACK
+HALF = 512
+HALVES = S2 // HALF
+BLOCKS = HALF // P
+RUN = 4
+VECTOR_COLS = 128
+OUT_BLOCKS = 1 + S2 // P
+
+FLOPS = 2 * TOK * F0 * FK * (S1 + S2)
+
+
+def regroup(copy, grouped, raw):
+    copy(
+        out=grouped.rearrange("p (q i) t -> p q t i", i=RUN),
+        in_=raw.rearrange("p t (q i) -> p q t i", i=RUN),
+    )
+
+
+def tile_cin_pa_s_kernel(tc, x, x1, w1, b1, w2, b2, out):
+    nc = tc.nc
+    with ExitStack() as ctx:
+        keep = ctx.enter_context(tc.tile_pool(name="keep", bufs=1))
+        psum = ctx.enter_context(tc.psum_pool(name="psum", bufs=1))
+        ctx.enter_context(tc.manual_schedule())
+
+        bias_rows = keep.tile([P, P], BF16)
+        nc.vector.memset(bias_rows[:], 0.0)
+        pooled = keep.tile([P, P], F32)
+        nc.vector.memset(pooled[:], 0.0)
+        pooled_bk = pooled[:, 0 : B * OUT_BLOCKS].rearrange("p (b k) -> p b k", k=OUT_BLOCKS)
+        ident_bf = keep.tile([P, P], BF16)
+        make_identity(nc, ident_bf[:])
+
+        x_cols = keep.tile([P, D // 2], BF16)
+        x_halves = x.rearrange("b i (h l) -> h (b i) l", h=2)
+        for h in range(2):
+            nc.sync.dma_start(out=x_cols[h * 64 : (h + 1) * 64, :], in_=x_halves[h])
+        x1_t = keep.tile([P, B, D], BF16)
+        nc.sync.dma_start(out=x1_t[:], in_=x1.rearrange("b j d -> j b d"))
+        w2_rows = w2.rearrange("(c t p) n -> c p t n", t=PACK, p=P)
+        w2_raw = {}
+
+        def load_w2(c, h):
+            w2_raw[c, h] = keep.tile([P, PACK, HALF], BF16, name="w2_raw_%d_%d" % (c, h))
+            nc.sync.dma_start(out=w2_raw[c, h][:], in_=w2_rows[c][:, :, h * HALF : (h + 1) * HALF])
+
+        load_w2(0, 0)
+        w1_raw = keep.tile([P, PASSES, PACK, S1], BF16)
+        nc.sync.dma_start(out=w1_raw[:], in_=w1.rearrange("(c t p) n -> p c t n", t=PACK, p=P))
+        nc.sync.dma_start(out=bias_rows[0:1, :], in_=b1.rearrange("(o s) -> o s", o=1))
+        nc.sync.dma_start(out=bias_rows[1:OUT_BLOCKS, :], in_=b2.rearrange("(k s) -> k s", s=P))
+        load_w2(1, 0)
+        load_w2(0, 1)
+        load_w2(1, 1)
+
+        w2_grouped = {}
+        w2_codes = {}
+        w2_scales = {}
+
+        def regroup_w2(c, h):
+            w2_grouped[c, h] = keep.tile([P, HALF, PACK], BF16, align_bytes=64, name="w2_grouped_%d_%d" % (c, h))
+            regroup(nc.vector.tensor_copy, w2_grouped[c, h][:, 0:VECTOR_COLS, :], w2_raw[c, h][:, :, 0:VECTOR_COLS])
+            regroup(nc.scalar.copy, w2_grouped[c, h][:, VECTOR_COLS:HALF, :], w2_raw[c, h][:, :, VECTOR_COLS:HALF])
+
+        def quantise_w2(c, h):
+            w2_codes[c, h] = keep.tile([P, HALF], U32, align_bytes=64, name="w2_codes_%d_%d" % (c, h))
+            w2_scales[c, h] = keep.tile([P, HALF], U8, align_bytes=64, name="w2_scales_%d_%d" % (c, h))
+            nc.vector.quantize_mx(
+                out=w2_codes[c, h][:].bitcast(FP8X4),
+                scales=w2_scales[c, h][:],
+                in_=w2_grouped[c, h][:].rearrange("p n t -> p (n t)"),
+            )
+
+        def times_x(name, maps):
+            z = keep.tile([P, PASSES, TOK, PACK], BF16, align_bytes=64, name=name)
+            nc.vector.tensor_tensor(
+                out=z[:],
+                in0=maps.unsqueeze(1).unsqueeze(3).to_broadcast([P, PASSES, TOK, PACK]),
+                in1=x_all[:].rearrange("p b h l (c t) -> p c (b h l) t", c=PASSES),
+                op=MULT,
+            )
+            return z
+
+        def quantise_both_passes(name, grouped):
+            codes = keep.tile([P, PASSES, P], U32, align_bytes=64, name=name + "_codes")
+            scales = keep.tile([P, PASSES, P], U8, align_bytes=64, name=name + "_scales")
+            nc.vector.quantize_mx(
+                out=codes[:].rearrange("p c n -> p (c n)").bitcast(FP8X4),
+                scales=scales[:].rearrange("p c n -> p (c n)"),
+                in_=grouped[:].rearrange("p c n t -> p (c n t)"),
+            )
+            return codes, scales
+
+        acc2 = {}
+
+        def multiply_half(h):
+            acc2[h] = psum.tile([P, BLOCKS, TOK], F32, name="acc2_%d" % h)
+            for k in range(BLOCKS):
+                cols = slice(k * P, (k + 1) * P)
+                for c in range(PASSES):
+                    nc.tensor.matmul_mx(
+                        out=acc2[h][:, k, :],
+                        lhsT=w2_codes[c, h][:, cols].bitcast(FP8X4),
+                        lhsT_scale=w2_scales[c, h][:, cols],
+                        rhs=z2_codes[:, c, :].bitcast(FP8X4),
+                        rhs_scale=z2_scales[:, c, :],
+                        start=(c == 0),
+                        stop=(c == PASSES - 1),
+                    )
+
+        def pool_half(h):
+            sums = keep.tile([P, B, BLOCKS], F32, name="sums_%d" % h)
+            nc.vector.tensor_reduce(
+                out=sums[:].rearrange("p b k -> p k b"),
+                in_=acc2[h][:].rearrange("p k (b d) -> p k b d", d=D),
+                axis=mybir.AxisListType.X,
+                op=ADD,
+            )
+            first = 1 + h * BLOCKS
+            nc.vector.scalar_tensor_tensor(
+                out=pooled_bk[:, :, first : first + BLOCKS],
+                in0=bias_cols[:, first : first + BLOCKS].unsqueeze(1).to_broadcast([P, B, BLOCKS]),
+                scalar=float(D),
+                in1=sums[:],
+                op0=MULT,
+                op1=ADD,
+            )
+
+        x_all = psum.tile([P, B, 2, D // 2, F0], BF16)
+        for l in range(D // 2):
+            nc.tensor.transpose(
+                out=x_all[:, :, :, l, :].rearrange("p b h i -> p h b i"),
+                in_=x_cols[:, l : l + 1].to_broadcast([P, P]),
+                identity=ident_bf[:],
+            )
+        bias_ps = psum.tile([P, P], BF16)
+        nc.tensor.transpose(out=bias_ps[:], in_=bias_rows[:], identity=ident_bf[:])
+
+        regroup_w2(0, 0)
+        w1_grouped = keep.tile([P, PASSES, S1, PACK], BF16, align_bytes=64)
+        for c in range(PASSES):
+            regroup(nc.vector.tensor_copy, w1_grouped[:, c], w1_raw[:, c])
+        bias_cols = keep.tile([P, OUT_BLOCKS], F32)
+        nc.scalar.copy(out=bias_cols[:], in_=bias_ps[:, 0:OUT_BLOCKS])
+        ident_f32 = keep.tile([P, P], F32)
+        nc.scalar.copy(out=ident_f32[:], in_=ident_bf[:])
+        z1 = times_x("z1", x1_t[:].rearrange("p b d -> p (b d)"))
+        w1_codes, w1_scales = quantise_both_passes("w1", w1_grouped)
+        z1_codes, z1_scales = quantise_both_passes("z1", z1)
+        acc1 = psum.tile([P, TOK], F32)
+        for c in range(PASSES):
+            nc.tensor.matmul_mx(
+                out=acc1[:],
+                lhsT=w1_codes[:, c, :].bitcast(FP8X4),
+                lhsT_scale=w1_scales[:, c, :],
+                rhs=z1_codes[:, c, :].bitcast(FP8X4),
+                rhs_scale=z1_scales[:, c, :],
+                start=(c == 0),
+                stop=(c == PASSES - 1),
+            )
+        quantise_w2(0, 0)
+
+        o1 = keep.tile([P, TOK], F32)
+        nc.vector.tensor_scalar_add(out=o1[:], in0=acc1[:], scalar1=bias_cols[:, 0:1])
+        z2 = times_x("z2", o1[:])
+        regroup_w2(1, 0)
+        z2_codes, z2_scales = quantise_both_passes("z2", z2)
+        quantise_w2(1, 0)
+        multiply_half(0)
+        regroup_w2(0, 1)
+        regroup_w2(1, 1)
+        quantise_w2(0, 1)
+        quantise_w2(1, 1)
+        multiply_half(1)
+
+        nc.vector.tensor_reduce(
+            out=pooled_bk[:, :, 0],
+            in_=o1[:].rearrange("p (b d) -> p b d", d=D),
+            axis=mybir.AxisListType.X,
+            op=ADD,
+        )
+        pool_half(0)
+        pool_half(1)
+
+        out_ps = psum.tile([P, P], F32)
+        nc.tensor.transpose(out=out_ps[:], in_=pooled[:], identity=ident_f32[:])
+        out_sb = keep.tile([P, P], F32)
+        nc.vector.tensor_copy(out=out_sb[:], in_=out_ps[:])
+        out_rows = out.rearrange("b (k s) -> (b k) s", s=P)
+        nc.sync.dma_start(out=out_rows[0:64, :], in_=out_sb[0:64, :])
+        nc.sync.dma_start(out=out_rows[64 : B * OUT_BLOCKS, :], in_=out_sb[64 : B * OUT_BLOCKS, :])

@@ -76,7 +76,14 @@ def tile_cin_pa_s_kernel(tc, x, x1, w1, b1, w2, b2, out):
 
         def regroup_w2(c, h):
             w2_grouped[c, h] = keep.tile([P, HALF, PACK], BF16, align_bytes=64, name="w2_grouped_%d_%d" % (c, h))
-            regroup(nc.vector.tensor_copy, w2_grouped[c, h][:, 0:VECTOR_COLS, :], w2_raw[c, h][:, :, 0:VECTOR_COLS])
+            nc.gpsimd.tensor_scalar(
+                out=w2_grouped[c, h][:, 0:VECTOR_COLS, :],
+                in0=w2_raw[c, h][:, :, 0:VECTOR_COLS].rearrange("p t n -> p n t"),
+                scalar1=1.0,
+                scalar2=0.0,
+                op0=MULT,
+                op1=ADD,
+            )
             regroup(nc.scalar.copy, w2_grouped[c, h][:, VECTOR_COLS:HALF, :], w2_raw[c, h][:, :, VECTOR_COLS:HALF])
 
         def quantise_w2(c, h):

@@ -18,9 +18,10 @@ TOK = B * D
 PASSES = F0 // PACK
 HALF = 512
 HALVES = S2 // HALF
-BLOCKS = HALF // P
+GROUP_COLS = (512, 256, 128, 128)
+GROUP_START = (0, 512, 768, 896)
 RUN = 4
-VECTOR_COLS = 128
+VECTOR_SHARE = 4
 OUT_BLOCKS = 1 + S2 // P
 
 FLOPS = 2 * TOK * F0 * FK * (S1 + S2)
@@ -70,29 +71,25 @@ def tile_cin_pa_s_kernel(tc, x, x1, w1, b1, w2, b2, out):
         load_w2(0, 1)
         load_w2(1, 1)
 
-        w2_grouped = {}
-        w2_codes = {}
-        w2_scales = {}
+        w2_grouped = [keep.tile([P, S2, PACK], BF16, align_bytes=64, name="w2_grouped_%d" % c) for c in range(PASSES)]
+        w2_codes = [keep.tile([P, S2], U32, align_bytes=64, name="w2_codes_%d" % c) for c in range(PASSES)]
+        w2_scales = [keep.tile([P, S2], U8, align_bytes=64, name="w2_scales_%d" % c) for c in range(PASSES)]
 
-        def regroup_w2(c, h):
-            w2_grouped[c, h] = keep.tile([P, HALF, PACK], BF16, align_bytes=64, name="w2_grouped_%d_%d" % (c, h))
-            nc.gpsimd.tensor_scalar(
-                out=w2_grouped[c, h][:, 0:VECTOR_COLS, :],
-                in0=w2_raw[c, h][:, :, 0:VECTOR_COLS].rearrange("p t n -> p n t"),
-                scalar1=1.0,
-                scalar2=0.0,
-                op0=MULT,
-                op1=ADD,
-            )
-            regroup(nc.scalar.copy, w2_grouped[c, h][:, VECTOR_COLS:HALF, :], w2_raw[c, h][:, :, VECTOR_COLS:HALF])
+        def regroup_w2(c, g):
+            start = GROUP_START[g]
+            split = start + GROUP_COLS[g] // VECTOR_SHARE
+            end = start + GROUP_COLS[g]
+            raw = w2_raw[c, start // HALF]
+            first = (start // HALF) * HALF
+            regroup(nc.vector.tensor_copy, w2_grouped[c][:, start:split, :], raw[:, :, start - first : split - first])
+            regroup(nc.scalar.copy, w2_grouped[c][:, split:end, :], raw[:, :, split - first : end - first])
 
-        def quantise_w2(c, h):
-            w2_codes[c, h] = keep.tile([P, HALF], U32, align_bytes=64, name="w2_codes_%d_%d" % (c, h))
-            w2_scales[c, h] = keep.tile([P, HALF], U8, align_bytes=64, name="w2_scales_%d_%d" % (c, h))
+        def quantise_w2(c, g):
+            cols = slice(GROUP_START[g], GROUP_START[g] + GROUP_COLS[g])
             nc.vector.quantize_mx(
-                out=w2_codes[c, h][:].bitcast(FP8X4),
-                scales=w2_scales[c, h][:],
-                in_=w2_grouped[c, h][:].rearrange("p n t -> p (n t)"),
+                out=w2_codes[c][:, cols].bitcast(FP8X4),
+                scales=w2_scales[c][:, cols],
+                in_=w2_grouped[c][:, cols, :].rearrange("p n t -> p (n t)"),
             )
 
         def times_x(name, maps):
@@ -117,33 +114,34 @@ def tile_cin_pa_s_kernel(tc, x, x1, w1, b1, w2, b2, out):
 
         acc2 = {}
 
-        def multiply_half(h):
-            acc2[h] = psum.tile([P, BLOCKS, TOK], F32, name="acc2_%d" % h)
-            for k in range(BLOCKS):
-                cols = slice(k * P, (k + 1) * P)
+        def multiply_group(g):
+            acc2[g] = psum.tile([P, GROUP_COLS[g] // P, TOK], F32, name="acc2_%d" % g)
+            for k in range(GROUP_COLS[g] // P):
+                cols = slice(GROUP_START[g] + k * P, GROUP_START[g] + (k + 1) * P)
                 for c in range(PASSES):
                     nc.tensor.matmul_mx(
-                        out=acc2[h][:, k, :],
-                        lhsT=w2_codes[c, h][:, cols].bitcast(FP8X4),
-                        lhsT_scale=w2_scales[c, h][:, cols],
+                        out=acc2[g][:, k, :],
+                        lhsT=w2_codes[c][:, cols].bitcast(FP8X4),
+                        lhsT_scale=w2_scales[c][:, cols],
                         rhs=z2_codes[:, c, :].bitcast(FP8X4),
                         rhs_scale=z2_scales[:, c, :],
                         start=(c == 0),
                         stop=(c == PASSES - 1),
                     )
 
-        def pool_half(h):
-            sums = keep.tile([P, B, BLOCKS], F32, name="sums_%d" % h)
+        def pool_group(g):
+            blocks = GROUP_COLS[g] // P
+            sums = keep.tile([P, B, blocks], F32, name="sums_%d" % g)
             nc.vector.tensor_reduce(
                 out=sums[:].rearrange("p b k -> p k b"),
-                in_=acc2[h][:].rearrange("p k (b d) -> p k b d", d=D),
+                in_=acc2[g][:].rearrange("p k (b d) -> p k b d", d=D),
                 axis=mybir.AxisListType.X,
                 op=ADD,
             )
-            first = 1 + h * BLOCKS
+            first = 1 + GROUP_START[g] // P
             nc.vector.scalar_tensor_tensor(
-                out=pooled_bk[:, :, first : first + BLOCKS],
-                in0=bias_cols[:, first : first + BLOCKS].unsqueeze(1).to_broadcast([P, B, BLOCKS]),
+                out=pooled_bk[:, :, first : first + blocks],
+                in0=bias_cols[:, first : first + blocks].unsqueeze(1).to_broadcast([P, B, blocks]),
                 scalar=float(D),
                 in1=sums[:],
                 op0=MULT,
@@ -190,26 +188,26 @@ def tile_cin_pa_s_kernel(tc, x, x1, w1, b1, w2, b2, out):
         regroup_w2(1, 0)
         z2_codes, z2_scales = quantise_both_passes("z2", z2)
         quantise_w2(1, 0)
-        multiply_half(0)
-        regroup_w2(0, 1)
-        regroup_w2(1, 1)
-        quantise_w2(0, 1)
-        quantise_w2(1, 1)
-        multiply_half(1)
-
+        multiply_group(0)
         nc.vector.tensor_reduce(
             out=pooled_bk[:, :, 0],
             in_=o1[:].rearrange("p (b d) -> p b d", d=D),
             axis=mybir.AxisListType.X,
             op=ADD,
         )
-        pool_half(0)
-        pool_half(1)
+        for g in range(1, len(GROUP_COLS)):
+            for c in range(PASSES):
+                regroup_w2(c, g)
+            for c in range(PASSES):
+                quantise_w2(c, g)
+            multiply_group(g)
+            pool_group(g - 1)
+        pool_group(len(GROUP_COLS) - 1)
 
         out_ps = psum.tile([P, P], F32)
         nc.tensor.transpose(out=out_ps[:], in_=pooled[:], identity=ident_f32[:])
         out_sb = keep.tile([P, P], F32)
-        nc.vector.tensor_copy(out=out_sb[:], in_=out_ps[:])
+        nc.scalar.copy(out=out_sb[:], in_=out_ps[:])
         out_rows = out.rearrange("b (k s) -> (b k) s", s=P)
         nc.sync.dma_start(out=out_rows[0:64, :], in_=out_sb[0:64, :])
         nc.sync.dma_start(out=out_rows[64 : B * OUT_BLOCKS, :], in_=out_sb[64 : B * OUT_BLOCKS, :])

from contextlib import ExitStack

import concourse.mybir as mybir
from concourse.masks import make_identity

BF16 = mybir.dt.bfloat16
F32 = mybir.dt.float32
U32 = mybir.dt.uint32
U8 = mybir.dt.uint8
FP8X4 = mybir.dt.float8_e4m3fn_x4
ADD = mybir.AluOpType.add
MULT = mybir.AluOpType.mult

P = 128
PACK = 4
B, F0, FK, S1, S2, D = 8, 8, 128, 128, 1024, 16
TOK = B * D
PASSES = F0 // PACK
HALF = 512
HALVES = S2 // HALF
GROUP_COLS = (512, 256, 128, 128)
GROUP_START = (0, 512, 768, 896)
RUN = 4
VECTOR_SHARE = 4
OUT_BLOCKS = 1 + S2 // P

FLOPS = 2 * TOK * F0 * FK * (S1 + S2)


def regroup(copy, grouped, raw):
    copy(
        out=grouped.rearrange("p (q i) t -> p q t i", i=RUN),
        in_=raw.rearrange("p t (q i) -> p q t i", i=RUN),
    )


def tile_cin_pa_s_kernel(tc, x, x1, w1, b1, w2, b2, out):
    nc = tc.nc
    with ExitStack() as ctx:
        keep = ctx.enter_context(tc.tile_pool(name="keep", bufs=1))
        psum = ctx.enter_context(tc.psum_pool(name="psum", bufs=1))
        ctx.enter_context(tc.manual_schedule())

        bias_rows = keep.tile([P, P], BF16)
        nc.vector.memset(bias_rows[:], 0.0)
        pooled = keep.tile([P, P], F32)
        nc.vector.memset(pooled[:], 0.0)
        pooled_bk = pooled[:, 0 : B * OUT_BLOCKS].rearrange("p (b k) -> p b k", k=OUT_BLOCKS)
        ident_bf = keep.tile([P, P], BF16)
        make_identity(nc, ident_bf[:])

        x_cols = keep.tile([P, D // 2], BF16)
        x_halves = x.rearrange("b i (h l) -> h (b i) l", h=2)
        for h in range(2):
            nc.sync.dma_start(out=x_cols[h * 64 : (h + 1) * 64, :], in_=x_halves[h])
        x1_t = keep.tile([P, B, D], BF16)
        nc.sync.dma_start(out=x1_t[:], in_=x1.rearrange("b j d -> j b d"))
        w2_rows = w2.rearrange("(c t p) n -> c p t n", t=PACK, p=P)
        w2_raw = {}

        def load_w2(c, h):
            w2_raw[c, h] = keep.tile([P, PACK, HALF], BF16, name="w2_raw_%d_%d" % (c, h))
            nc.sync.dma_start(out=w2_raw[c, h][:], in_=w2_rows[c][:, :, h * HALF : (h + 1) * HALF])

        load_w2(0, 0)
        w1_raw = keep.tile([P, PASSES, PACK, S1], BF16)
        nc.sync.dma_start(out=w1_raw[:], in_=w1.rearrange("(c t p) n -> p c t n", t=PACK, p=P))
        nc.sync.dma_start(out=bias_rows[0:1, :], in_=b1.rearrange("(o s) -> o s", o=1))
        nc.sync.dma_start(out=bias_rows[1:OUT_BLOCKS, :], in_=b2.rearrange("(k s) -> k s", s=P))
        load_w2(1, 0)
        load_w2(0, 1)
        load_w2(1, 1)

        w2_grouped = [keep.tile([P, S2, PACK], BF16, align_bytes=64, name="w2_grouped_%d" % c) for c in range(PASSES)]
        w2_codes = [keep.tile([P, S2], U32, align_bytes=64, name="w2_codes_%d" % c) for c in range(PASSES)]
        w2_scales = [keep.tile([P, S2], U8, align_bytes=64, name="w2_scales_%d" % c) for c in range(PASSES)]

        def regroup_w2(c, g):
            start = GROUP_START[g]
            split = start + GROUP_COLS[g] // VECTOR_SHARE
            end = start + GROUP_COLS[g]
            raw = w2_raw[c, start // HALF]
            first = (start // HALF) * HALF
            regroup(nc.vector.tensor_copy, w2_grouped[c][:, start:split, :], raw[:, :, start - first : split - first])
            regroup(nc.scalar.copy, w2_grouped[c][:, split:end, :], raw[:, :, split - first : end - first])

        def quantise_w2(c, g):
            cols = slice(GROUP_START[g], GROUP_START[g] + GROUP_COLS[g])
            nc.vector.quantize_mx(
                out=w2_codes[c][:, cols].bitcast(FP8X4),
                scales=w2_scales[c][:, cols],
                in_=w2_grouped[c][:, cols, :].rearrange("p n t -> p (n t)"),
            )

        def times_x(name, maps):
            z = keep.tile([P, PASSES, TOK, PACK], BF16, align_bytes=64, name=name)
            nc.vector.tensor_tensor(
                out=z[:],
                in0=maps.unsqueeze(1).unsqueeze(3).to_broadcast([P, PASSES, TOK, PACK]),
                in1=x_all[:].rearrange("p b h l (c t) -> p c (b h l) t", c=PASSES),
                op=MULT,
            )
            return z

        def quantise_both_passes(name, grouped):
            codes = keep.tile([P, PASSES, P], U32, align_bytes=64, name=name + "_codes")
            scales = keep.tile([P, PASSES, P], U8, align_bytes=64, name=name + "_scales")
            nc.vector.quantize_mx(
                out=codes[:].rearrange("p c n -> p (c n)").bitcast(FP8X4),
                scales=scales[:].rearrange("p c n -> p (c n)"),
                in_=grouped[:].rearrange("p c n t -> p (c n t)"),
            )
            return codes, scales

        acc2 = {}

        def multiply_group(g):
            acc2[g] = psum.tile([P, GROUP_COLS[g] // P, TOK], F32, name="acc2_%d" % g)
            for k in range(GROUP_COLS[g] // P):
                cols = slice(GROUP_START[g] + k * P, GROUP_START[g] + (k + 1) * P)
                for c in range(PASSES):
                    nc.tensor.matmul_mx(
                        out=acc2[g][:, k, :],
                        lhsT=w2_codes[c][:, cols].bitcast(FP8X4),
                        lhsT_scale=w2_scales[c][:, cols],
                        rhs=z2_codes[:, c, :].bitcast(FP8X4),
                        rhs_scale=z2_scales[:, c, :],
                        start=(c == 0),
                        stop=(c == PASSES - 1),
                    )

        def pool_group(g):
            blocks = GROUP_COLS[g] // P
            sums = keep.tile([P, B, blocks], F32, name="sums_%d" % g)
            nc.vector.tensor_reduce(
                out=sums[:].rearrange("p b k -> p k b"),
                in_=acc2[g][:].rearrange("p k (b d) -> p k b d", d=D),
                axis=mybir.AxisListType.X,
                op=ADD,
            )
            first = 1 + GROUP_START[g] // P
            nc.vector.scalar_tensor_tensor(
                out=pooled_bk[:, :, first : first + blocks],
                in0=bias_cols[:, first : first + blocks].unsqueeze(1).to_broadcast([P, B, blocks]),
                scalar=float(D),
                in1=sums[:],
                op0=MULT,
                op1=ADD,
            )

        x_all = psum.tile([P, B, 2, D // 2, F0], BF16)
        for l in range(D // 2):
            nc.tensor.transpose(
                out=x_all[:, :, :, l, :].rearrange("p b h i -> p h b i"),
                in_=x_cols[:, l : l + 1].to_broadcast([P, P]),
                identity=ident_bf[:],
            )
        bias_ps = psum.tile([P, P], BF16)
        nc.tensor.transpose(out=bias_ps[:], in_=bias_rows[:], identity=ident_bf[:])

        regroup_w2(0, 0)
        w1_grouped = keep.tile([P, PASSES, S1, PACK], BF16, align_bytes=64)
        for c in range(PASSES):
            regroup(nc.vector.tensor_copy, w1_grouped[:, c], w1_raw[:, c])
        bias_cols = keep.tile([P, OUT_BLOCKS], F32)
        nc.scalar.copy(out=bias_cols[:], in_=bias_ps[:, 0:OUT_BLOCKS])
        ident_f32 = keep.tile([P, P], F32)
        nc.scalar.copy(out=ident_f32[:], in_=ident_bf[:])
        z1 = times_x("z1", x1_t[:].rearrange("p b d -> p (b d)"))
        w1_codes, w1_scales = quantise_both_passes("w1", w1_grouped)
        z1_codes, z1_scales = quantise_both_passes("z1", z1)
        acc1 = psum.tile([P, TOK], F32)
        for c in range(PASSES):
            nc.tensor.matmul_mx(
                out=acc1[:],
                lhsT=w1_codes[:, c, :].bitcast(FP8X4),
                lhsT_scale=w1_scales[:, c, :],
                rhs=z1_codes[:, c, :].bitcast(FP8X4),
                rhs_scale=z1_scales[:, c, :],
                start=(c == 0),
                stop=(c == PASSES - 1),
            )
        quantise_w2(0, 0)

        o1 = keep.tile([P, TOK], F32)
        nc.vector.tensor_scalar_add(out=o1[:], in0=acc1[:], scalar1=bias_cols[:, 0:1])
        z2 = times_x("z2", o1[:])
        regroup_w2(1, 0)
        z2_codes, z2_scales = quantise_both_passes("z2", z2)
        quantise_w2(1, 0)
        multiply_group(0)
        nc.vector.tensor_reduce(
            out=pooled_bk[:, :, 0],
            in_=o1[:].rearrange("p (b d) -> p b d", d=D),
            axis=mybir.AxisListType.X,
            op=ADD,
        )
        for g in range(1, len(GROUP_COLS)):
            for c in range(PASSES):
                regroup_w2(c, g)
            for c in range(PASSES):
                quantise_w2(c, g)
            multiply_group(g)
            pool_group(g - 1)
        pool_group(len(GROUP_COLS) - 1)

        out_ps = psum.tile([P, P], F32)
        nc.tensor.transpose(out=out_ps[:], in_=pooled[:], identity=ident_f32[:])
        out_sb = keep.tile([P, P], F32)
        nc.scalar.copy(out=out_sb[:], in_=out_ps[:])
        out_rows = out.rearrange("b (k s) -> (b k) s", s=P)
        nc.sync.dma_start(out=out_rows[0:64, :], in_=out_sb[0:64, :])
        nc.sync.dma_start(out=out_rows[64 : B * OUT_BLOCKS, :], in_=out_sb[64 : B * OUT_BLOCKS, :])
